import numpy as np
import ml_dtypes


def mxq(x, axis, fmt="e4m3"):
    dtype, down = {"e4m3": (ml_dtypes.float8_e4m3fn, 7), "e5m2": (ml_dtypes.float8_e5m2, 14)}[fmt]
    v = np.moveaxis(np.asarray(x, np.float32).astype(ml_dtypes.bfloat16).astype(np.float64), axis, -1)
    blocks = v.reshape(v.shape[:-1] + (-1, 32))
    amax = np.abs(blocks).max(-1, keepdims=True)
    byte = np.maximum(np.where(amax > 0, np.frexp(amax)[1] - 1 + 127, 0) - down, 1)
    scale = np.exp2(byte - 127.0)
    codes = (blocks / scale).astype(np.float32).astype(dtype).astype(np.float64)
    return np.moveaxis((codes * scale).reshape(v.shape), -1, axis)


WIDE = False


def mx_kscale(k):
    if not WIDE:
        return np.ones(k)
    levels = np.array([10, -10, 5, -5, 0])
    if k % 512:
        return np.exp2(np.random.permutation(np.resize(levels, k // 32))).repeat(32)
    a = np.empty((k // 512, 16))
    for p in range(k // 512):
        a[p, :8] = np.random.permutation(np.resize(levels, 8))
        for g in range(8):
            far = levels[np.abs(levels - a[p, g]) >= 10]
            a[p, g + 8] = far[np.random.randint(len(far))]
    return np.exp2(a.ravel()).repeat(32)


BF16 = ml_dtypes.bfloat16


def bf(x):
    return np.asarray(x, np.float32).astype(BF16)


def f64(x):
    return np.asarray(x).astype(np.float64)


E2M1 = np.array([0.0, 0.5, 1.0, 1.5, 2.0, 3.0, 4.0, 6.0, -0.0, -0.5, -1.0, -1.5, -2.0, -3.0, -4.0, -6.0])


def pack_weight(w, fmt):
    k, n = w.shape
    w = f64(bf(w)).reshape(k // 32, 32, n)
    amax = np.abs(w).max(1)
    if fmt == "e4m3":
        byte = np.frexp(amax)[1] - 1 + 127 - 7
    else:
        mant, ex = np.frexp(amax / 6.0)
        byte = np.where(mant > 0.5, ex, ex - 1) + 127
    byte = np.clip(np.where(amax > 0, byte, 1), 1, 254)
    scaled = (w * np.exp2(127.0 - byte)[:, None, :]).reshape(k, n).astype(np.float32)
    by_word = np.ascontiguousarray(scaled.reshape(k // 512, 128, 4, n).transpose(0, 1, 3, 2))
    if fmt == "e4m3":
        words = by_word.astype(ml_dtypes.float8_e4m3fn).view(np.uint8)
    else:
        c = by_word.astype(ml_dtypes.float4_e2m1fn).view(np.uint8) & 0xF
        words = c[..., 0::2] | (c[..., 1::2] << 4)
    return np.ascontiguousarray(words), np.ascontiguousarray(byte.astype(np.uint8).reshape(k // 512, 16, n))


def unpack_weight(words, scales, fmt):
    g, p, n, _ = words.shape
    if fmt == "e4m3":
        vals = np.ascontiguousarray(words).view(ml_dtypes.float8_e4m3fn).astype(np.float64)
    else:
        nib = np.empty((g, p, n, 4), np.uint8)
        nib[..., 0::2] = words & 0xF
        nib[..., 1::2] = words >> 4
        vals = E2M1[nib]
    vals = vals * np.repeat(np.exp2(scales.astype(np.float64) - 127.0), 8, axis=1)[..., None]
    return vals.transpose(0, 1, 3, 2).reshape(g * 512, n)
def pack4(w):
    words, scales = pack_weight(w, "e2m1")
    return words.reshape(words.shape[0], 128, -1), scales


def unpack4(words, scales):
    return unpack_weight(words.reshape(words.shape[0], 128, -1, 2), scales, "e2m1")


B_, S, D_IN, D_OUT, N, RANK, ALPHA = 4, 2048, 512, 256, 32, 16, 32
NR = N * RANK
SCALE = ALPHA / RANK


def draw0():
    s, t = mx_kscale(D_IN), mx_kscale(NR)
    tn = t.reshape(N, RANK)
    x = bf(np.random.standard_normal((B_, S, D_IN)) * s)
    lora_A = bf(np.random.standard_normal((N, RANK, D_IN)) / np.sqrt(D_IN) / s * tn[:, :, None])
    lora_B = bf(np.random.standard_normal((N, D_OUT, RANK)) / np.sqrt(RANK) / tn[:, None, :])
    W_words, W_scales = pack4((np.random.standard_normal((D_OUT, D_IN)) / np.sqrt(D_IN) / s).T)
    return {"x": x,
            "lora_A": lora_A,
            "lora_B": lora_B,
            "W_words": W_words,
            "W_scales": W_scales,
            "bias": bf(np.random.standard_normal(D_OUT) * 0.3),
            "lora_weights": bf((1.0 + 0.5 * np.random.standard_normal(N)) * 2.0 / N)}


def core(x, lora_A, lora_B, W_words, W_scales, bias, lora_weights):
    xq = mxq(f64(x), 2, "e4m3")
    h = xq @ mxq(f64(lora_A).reshape(NR, D_IN), 1, "e4m3").T
    coef = (SCALE * f64(lora_weights))[:, None, None]
    bc = (f64(lora_B) * coef).transpose(1, 0, 2).reshape(D_OUT, NR)
    lora_out = mxq(h, 2, "e4m3") @ mxq(bc, 1, "e4m3").T
    base = (xq @ unpack4(W_words, W_scales)) + f64(bias)
    return base + lora_out


def e4m3fn_bytes(y):
    return np.clip(np.asarray(y, np.float64), -448.0, 448.0).astype(np.float32).astype(ml_dtypes.float8_e4m3fn).view(np.uint8)


def e4m3fn_values(b):
    return np.asarray(b, np.uint8).view(ml_dtypes.float8_e4m3fn).astype(np.float64)


def setup_inputs():
    d = draw0()
    x0 = np.asarray(d['x']).astype(np.float64)
    s = (np.max(np.abs(x0), axis=(0, 1), keepdims=True) / 448.0).astype(np.float32)
    out = {}
    for k, v in d.items():
        if k == 'x':
            out['x_bytes'] = e4m3fn_bytes(x0 / s.astype(np.float64))
            out['x_scale'] = s
        else:
            out[k] = v
    return out


def reference(x_bytes, x_scale, lora_A, lora_B, W_words, W_scales, bias, lora_weights):
    return core(e4m3fn_values(x_bytes) * x_scale.astype(np.float64), lora_A, lora_B, W_words, W_scales, bias, lora_weights)

from contextlib import ExitStack

import concourse.mybir as mybir
from concourse.masks import make_identity

TOKENS, D, NR, D_OUT = 8192, 512, 512, 256
FLOPS = 2 * TOKENS * (D * NR + D * D_OUT + NR * D_OUT)

F32 = mybir.dt.float32
BF16 = mybir.dt.bfloat16
U32 = mybir.dt.uint32
I32 = mybir.dt.int32
U8 = mybir.dt.uint8
FP8 = mybir.dt.float8_e4m3fn
FP8X4 = mybir.dt.float8_e4m3fn_x4
FP4X4 = mybir.dt.float4_e2m1fn_x4
ALU = mybir.AluOpType
ACT = mybir.ActivationFunctionType

P = 128
PER = 8
CHUNKS = TOKENS // (P * PER)
PAIRS = TOKENS // (2 * P)
PPC = PER // 2


def tile_replaced_compose_lora_pa_t_w4_kernel(
    tc, x_bytes, x_scale, lora_A, lora_B, W_words, W_scales, bias, lora_weights, out
):
    nc = tc.nc
    x_rows = x_bytes.rearrange("b s d -> (b s) d").rearrange("(c p n) d -> c p (n d)", p=P, n=PER)
    out_rows = out.rearrange("b s o -> (b s) o").rearrange("(c p n) o -> c p n o", p=P, n=PER)

    with ExitStack() as ctx:
        keep = ctx.enter_context(tc.tile_pool(name="keep", bufs=1))
        work = ctx.enter_context(tc.tile_pool(name="work", bufs=1))
        psum = ctx.enter_context(tc.psum_pool(name="psum", bufs=1))
        ctx.enter_context(tc.manual_schedule())

        ident = keep.tile([P, P], F32, name="ident")
        make_identity(nc, ident[:])

        xb = [keep.tile([P, PER * D], U8, name="xb%d" % c, align_bytes=64) for c in range(CHUNKS)]
        scale = keep.tile([P, 2 * D], F32, name="scale", align_bytes=64)
        a_sb = keep.tile([P, 4 * D], BF16, name="a_sb", align_bytes=64)
        b_sb = keep.tile([P, 2, 32, 16], BF16, name="b_sb", align_bytes=64)
        w_sb = keep.tile([P, 2 * D_OUT], U8, name="w_sb", align_bytes=64)
        w_sc = keep.tile([P, D_OUT], U8, name="w_sc", align_bytes=64)
        bias_sb = keep.tile([P, D_OUT], BF16, name="bias_sb", align_bytes=64)
        lw_sb = keep.tile([P, 32], BF16, name="lw_sb", align_bytes=64)
        coef = keep.tile([P, 1], F32, name="coef")
        junk = keep.tile([P, P], F32, name="junk")
        warm = keep.tile([P, 1], F32, name="warm")

        nc.vector.memset(w_sc[:].bitcast(I32), 0)
        nc.vector.memset(warm[:], 0.0)
        nc.scalar.dma_start(out=scale[:, 0:D], in_=x_scale.rearrange("a b k -> (a b k)").partition_broadcast(P))
        nc.sync.dma_start(out=xb[0][:, 0 : 2 * D], in_=x_rows[0][:, 0 : 2 * D])
        nc.sync.dma_start(out=a_sb[:], in_=lora_A.rearrange("n r d -> (n r) d").rearrange("(m t) d -> m (t d)", t=4))
        nc.scalar.dma_start(out=lw_sb[:], in_=lora_weights.partition_broadcast(P))
        for h in range(2):
            nc.scalar.dma_start(out=b_sb[:, h], in_=lora_B[:, h * P : (h + 1) * P, :].rearrange("n o r -> o n r"))
        nc.scalar.dma_start(out=bias_sb[:], in_=bias.partition_broadcast(P))
        for q in range(1, PPC):
            nc.sync.dma_start(out=xb[0][:, q * 2 * D : (q + 1) * 2 * D], in_=x_rows[0][:, q * 2 * D : (q + 1) * 2 * D])
        nc.sync.dma_start(out=w_sb[:], in_=W_words[0])
        for q in range(4):
            nc.sync.dma_start(
                out=w_sc[32 * q : 32 * q + 4, :].bitcast(I32), in_=W_scales[0, 4 * q : 4 * q + 4, :].bitcast(I32)
            )
        for c in range(1, CHUNKS):
            nc.sync.dma_start(out=xb[c][:], in_=x_rows[c])

        nc.scalar.activation(out=warm[:], in_=warm[:], func=ACT.Copy, scale=1.0)

        a_codes = keep.tile([P, NR], U32, name="a_codes", align_bytes=64)
        a_scales = keep.tile([P, NR], U8, name="a_scales", align_bytes=64)
        b_codes = keep.tile([P, D_OUT], U32, name="b_codes", align_bytes=64)
        b_scales = keep.tile([P, D_OUT], U8, name="b_scales", align_bytes=64)
        a_grp = keep.tile([P, 4 * NR], BF16, name="a_grp", align_bytes=64)
        b_grp = keep.tile([P, 4 * D_OUT], BF16, name="b_grp", align_bytes=64)

        def turn(rows):
            words = rows.bitcast(F32)
            xt = psum.tile([P, 2, 2, P], F32, name="xt", tag="xt", bufs=2)
            for j in range(2):
                for u in range(2):
                    nc.tensor.transpose(xt[:, j, u, :], words[:, 256 * j + u : 256 * (j + 1) : 2], ident[:])
            return xt

        def empty_turned(xt, dst):
            nc.scalar.copy(
                out=dst.bitcast(F32).rearrange("p (j r u) -> p j r u", j=2, u=2),
                in_=xt[:].rearrange("p j u r -> p j r u"),
            )

        st = {}

        def widen(i):
            c, q = divmod(i, PPC)
            xw = work.tile([P, 2 * D], BF16, name="xw", tag="xw", bufs=4, align_bytes=64)
            nc.vector.tensor_tensor(
                out=xw[:],
                in0=xb[c][:, q * 2 * D : (q + 1) * 2 * D].bitcast(FP8),
                in1=scale[:],
                op=ALU.mult,
            )
            st["xw", i] = xw

        def t_stage(i):
            st["xt", i] = turn(st.pop(("xw", i))[:])

        def e_stage(i):
            xg = work.tile([P, 2 * D], BF16, name="xg", tag="xg", bufs=3, align_bytes=64)
            empty_turned(st.pop(("xt", i)), xg[:])
            st["xg", i] = xg

        def qx_stage(i):
            xg = st.pop(("xg", i))
            xc = work.tile([P, 2 * P], U32, name="xc", tag="xc", bufs=6, align_bytes=64)
            xs = work.tile([P, 2 * P], U8, name="xs", tag="xs", bufs=6, align_bytes=64)
            nc.vector.quantize_mx(out=xc[:].bitcast(FP8X4), scales=xs[:], in_=xg[:])
            st["xc", i] = (xc, xs)

        def h_stage(i):
            xc, xs = st["xc", i]
            hp = []
            for j in range(2):
                h = psum.tile([P, 4, P], F32, name="hp", tag="hp", bufs=4)
                cols = slice(j * P, (j + 1) * P)
                for t in range(4):
                    ch = slice(t * P, (t + 1) * P)
                    nc.tensor.matmul_mx(
                        out=h[:, t, :],
                        lhsT=a_codes[:, ch].bitcast(FP8X4),
                        lhsT_scale=a_scales[:, ch],
                        rhs=xc[:, cols].bitcast(FP8X4),
                        rhs_scale=xs[:, cols],
                        start=True,
                        stop=True,
                    )
                hp.append(h)
            st["hp", i] = hp

        def eh_stage(i):
            hp = st.pop(("hp", i))
            hg = work.tile([P, 2 * NR], BF16, name="hg", tag="hg", bufs=3, align_bytes=64)
            for j in range(2):
                nc.scalar.copy(
                    out=hg[:, j * NR : (j + 1) * NR].rearrange("p (r t) -> p r t", t=4),
                    in_=hp[j][:].rearrange("p t r -> p r t"),
                )
            st["hg", i] = hg

        def qh_stage(i):
            hg = st.pop(("hg", i))
            hc = work.tile([P, 2 * P], U32, name="hc", tag="hc", bufs=3, align_bytes=64)
            hs = work.tile([P, 2 * P], U8, name="hs", tag="hs", bufs=3, align_bytes=64)
            nc.vector.quantize_mx(out=hc[:].bitcast(FP8X4), scales=hs[:], in_=hg[:])
            st["hc", i] = (hc, hs)

        def o_stage(i):
            xc, xs = st.pop(("xc", i))
            hc, hs = st.pop(("hc", i))
            op = psum.tile([P, 2, D_OUT], F32, name="op", tag="op", bufs=2)
            for j in range(2):
                cols = slice(j * P, (j + 1) * P)
                for half in range(2):
                    oc = slice(half * P, (half + 1) * P)
                    nc.tensor.matmul_mx(
                        out=op[:, j, oc],
                        lhsT=xc[:, cols].bitcast(FP8X4),
                        lhsT_scale=xs[:, cols],
                        rhs=w_sb[:, half * 256 : (half + 1) * 256].bitcast(FP4X4),
                        rhs_scale=w_sc[:, oc],
                        start=True,
                        stop=False,
                    )
                    nc.tensor.matmul_mx(
                        out=op[:, j, oc],
                        lhsT=hc[:, cols].bitcast(FP8X4),
                        lhsT_scale=hs[:, cols],
                        rhs=b_codes[:, oc].bitcast(FP8X4),
                        rhs_scale=b_scales[:, oc],
                        start=False,
                        stop=True,
                    )
            st["op", i] = op

        def out_stage(i):
            c, q = divmod(i, PPC)
            op = st.pop(("op", i))
            ob = work.tile([P, 2, D_OUT], F32, name="ob", tag="ob", bufs=4, align_bytes=64)
            nc.vector.tensor_tensor(
                out=ob[:], in0=op[:], in1=bias_sb[:].unsqueeze(1).to_broadcast([P, 2, D_OUT]), op=ALU.add
            )
            nc.sync.dma_start(out=out_rows[c][:, 2 * q : 2 * q + 2, :], in_=ob[:])

        nc.scalar.copy(out=scale[:, D : 2 * D], in_=scale[:, 0:D])
        widen(0)
        a_t = [turn(a_sb[:, h * 2 * D : (h + 1) * 2 * D]) for h in range(2)]
        for h in range(2):
            empty_turned(a_t[h], a_grp[:, h * 2 * D : (h + 1) * 2 * D])
        nc.vector.scalar_tensor_tensor(
            out=junk[:].rearrange("p (n q) -> p n q", q=4),
            in0=ident[:].rearrange("p (n q) -> p n q", q=4),
            scalar=2.0,
            in1=lw_sb[:].unsqueeze(2).to_broadcast([P, 32, 4]),
            op0=ALU.mult,
            op1=ALU.mult,
            accum_out=coef[:],
        )

        for s in range(PAIRS + 5):
            if s + 1 < PAIRS:
                widen(s + 1)
            if s == 0:
                nc.vector.quantize_mx(out=a_codes[:].bitcast(FP8X4), scales=a_scales[:], in_=a_grp[:])
            if 0 <= s - 1 < PAIRS:
                qx_stage(s - 1)
            if 0 <= s - 5 < PAIRS:
                out_stage(s - 5)
            if 0 <= s - 3 < PAIRS:
                qh_stage(s - 3)
            if s == 2:
                nc.vector.quantize_mx(out=b_codes[:].bitcast(FP8X4), scales=b_scales[:], in_=b_grp[:])
            if s < PAIRS:
                t_stage(s)
                e_stage(s)
            if 0 <= s - 2 < PAIRS:
                h_stage(s - 2)
                eh_stage(s - 2)
            if s == 1:
                b_t = turn(b_sb[:].rearrange("p h n r -> p (h n r)"))
                for h in range(2):
                    nc.scalar.activation(
                        out=b_grp[:, h * 2 * D_OUT : (h + 1) * 2 * D_OUT].rearrange("p (r u e) -> p r u e", u=2, e=2),
                        in_=b_t[:, h].bitcast(BF16).rearrange("p u (r e) -> p r u e", e=2),
                        func=ACT.Copy,
                        scale=coef[:],
                    )
            if 0 <= s - 4 < PAIRS:
                o_stage(s - 4)
